import numpy as np
import ml_dtypes


def mxq(x, axis, fmt="e4m3"):
    dtype, down = {"e4m3": (ml_dtypes.float8_e4m3fn, 7), "e5m2": (ml_dtypes.float8_e5m2, 14)}[fmt]
    v = np.moveaxis(np.asarray(x, np.float32).astype(ml_dtypes.bfloat16).astype(np.float64), axis, -1)
    blocks = v.reshape(v.shape[:-1] + (-1, 32))
    amax = np.abs(blocks).max(-1, keepdims=True)
    byte = np.maximum(np.where(amax > 0, np.frexp(amax)[1] - 1 + 127, 0) - down, 1)
    scale = np.exp2(byte - 127.0)
    codes = (blocks / scale).astype(np.float32).astype(dtype).astype(np.float64)
    return np.moveaxis((codes * scale).reshape(v.shape), -1, axis)


WIDE = False


def mx_kscale(k):
    if not WIDE:
        return np.ones(k)
    levels = np.array([10, -10, 5, -5, 0])
    a = np.random.permutation(np.resize(levels, k // 512 * 4)).reshape(k // 512, 4)
    idx = np.arange(k)
    return np.exp2(a[idx // 512, idx % 128 // 32])


BF16 = ml_dtypes.bfloat16


def bf(x):
    return np.asarray(x, np.float32).astype(BF16)


def f64(x):
    return np.asarray(x).astype(np.float64)


B, S, H, NH, LAT = 2, 64, 8192, 16, 512
HD = H // NH
HALF = H // 2
R = HALF // 2
ROPE_BASE = 10000.0


def rope_table():
    inv_freq = 1.0 / ROPE_BASE ** (np.arange(0, R, 2) / R)
    freqs = np.outer(np.arange(S), inv_freq)
    emb = np.concatenate([freqs, freqs], -1)
    return np.cos(emb), np.sin(emb)


def apply_rotary(x, cos, sin):
    h = x.shape[-1] // 2
    x1, x2 = x[..., :h], x[..., h:]
    return np.concatenate([x1 * cos - x2 * sin, x1 * sin + x2 * cos], -1)


def setup_inputs():
    s, t = mx_kscale(H), mx_kscale(LAT)
    cos, sin = rope_table()
    return {"hidden_states": bf(np.random.standard_normal((B, S, H)) * s),
            "Wkv_down": bf(np.random.standard_normal((LAT, H)) / np.sqrt(H) * t[:, None] / s),
            "bkv_down": bf(np.random.standard_normal(LAT) * 0.2 * t),
            "Wk_up": bf(np.random.standard_normal((HALF, LAT)) * 1.2 / np.sqrt(LAT) / t),
            "bk_up": bf(np.random.standard_normal(HALF) * 0.2),
            "Wv_up": bf(np.random.standard_normal((H, LAT)) / np.sqrt(LAT) / t),
            "bv_up": bf(np.random.standard_normal(H) * 0.2),
            "rope_cos": bf(cos),
            "rope_sin": bf(sin)}


def reference(hidden_states, Wkv_down, bkv_down, Wk_up, bk_up, Wv_up, bv_up, rope_cos, rope_sin):
    kv_lat = (mxq(f64(hidden_states), 2, "e4m3") @ mxq(f64(Wkv_down), 1, "e4m3").T) + f64(bkv_down)
    lat_q = mxq(kv_lat, 2, "e4m3")
    k_half = (lat_q @ mxq(f64(Wk_up), 1, "e4m3").T) + f64(bk_up)
    k = np.concatenate([k_half, apply_rotary(k_half, f64(rope_cos), f64(rope_sin))], -1)
    v = (lat_q @ mxq(f64(Wv_up), 1, "e4m3").T) + f64(bv_up)
    k = k.reshape(B, S, NH, HD).transpose(0, 2, 1, 3)
    v = v.reshape(B, S, NH, HD).transpose(0, 2, 1, 3)
    return k, v

@@ -1,0 +1,255 @@
+from contextlib import ExitStack
+
+import concourse.mybir as mybir
+from concourse.masks import make_identity
+
+F32 = mybir.dt.float32
+BF16 = mybir.dt.bfloat16
+U32 = mybir.dt.uint32
+U8 = mybir.dt.uint8
+FP8X4 = mybir.dt.float8_e4m3fn_x4
+ADD = mybir.AluOpType.add
+SUBTRACT = mybir.AluOpType.subtract
+MULT = mybir.AluOpType.mult
+
+P = 128
+BATCH, SEQ, HIDDEN, LATENT = 2, 64, 8192, 512
+HEAD = 512
+KEY_HALF = 4096
+VALUE = 8192
+CHUNK = 4096
+RUN = 512
+RUNS = CHUNK // RUN
+BANK_WORDS = 512
+BIAS_ROW = 256
+LOAD_AHEAD = 12
+LAG = 1
+
+FLOPS = 2 * BATCH * SEQ * (HIDDEN * LATENT + LATENT * (KEY_HALF + VALUE))
+
+
+def tile_multiheadlatentattention_pb_k_kernel(
+    tc, hidden_states, Wkv_down, bkv_down, Wk_up, bk_up, Wv_up, bv_up, rope_cos, rope_sin, out_0, out_1
+):
+    nc = tc.nc
+    with ExitStack() as ctx:
+        keep = ctx.enter_context(tc.tile_pool(name="keep", bufs=1))
+        raw_pool = ctx.enter_context(tc.tile_pool(name="raw", bufs=LOAD_AHEAD))
+        grouped_pool = ctx.enter_context(tc.tile_pool(name="grouped", bufs=4))
+        code_pool = ctx.enter_context(tc.tile_pool(name="codes", bufs=3))
+        bias_pool = ctx.enter_context(tc.tile_pool(name="bias", bufs=3))
+        key_pool = ctx.enter_context(tc.tile_pool(name="key", bufs=2))
+        value_pool = ctx.enter_context(tc.tile_pool(name="value", bufs=3))
+        turned_psum = ctx.enter_context(tc.psum_pool(name="turned", bufs=4))
+        latent_psum = ctx.enter_context(tc.psum_pool(name="latent", bufs=1))
+        product_psum = ctx.enter_context(tc.psum_pool(name="product", bufs=3))
+
+        ident = keep.tile([P, P], F32)
+        make_identity(nc, ident[:])
+
+        key_bias_row = 0
+        value_bias_row = KEY_HALF // BIAS_ROW
+        latent_bias_row = value_bias_row + VALUE // BIAS_ROW
+        bias_table = keep.tile([P, BIAS_ROW], BF16)
+        nc.vector.memset(bias_table[:], 0.0)
+        nc.scalar.dma_start(
+            out=bias_table[key_bias_row:value_bias_row, :], in_=bk_up.rearrange("(m c) -> m c", c=BIAS_ROW)
+        )
+        nc.scalar.dma_start(
+            out=bias_table[value_bias_row:latent_bias_row, :], in_=bv_up.rearrange("(m c) -> m c", c=BIAS_ROW)
+        )
+        nc.scalar.dma_start(
+            out=bias_table[latent_bias_row : latent_bias_row + LATENT // BIAS_ROW, :],
+            in_=bkv_down.rearrange("(m c) -> m c", c=BIAS_ROW),
+        )
+        table_turned = turned_psum.tile([P, 4, P], F32, tag="turned")
+        nc.tensor.transpose(table_turned[:, 0, :], bias_table[:].bitcast(F32), ident[:])
+        bias_columns = keep.tile([P, P], F32)
+        nc.vector.tensor_copy(out=bias_columns[:], in_=table_turned[:, 0, :])
+        latent_bias = keep.tile([P, 4], F32)
+        nc.vector.tensor_copy(
+            out=latent_bias[:], in_=bias_columns[:, latent_bias_row : latent_bias_row + 2].bitcast(BF16)
+        )
+
+        x_codes = keep.tile([P, (HIDDEN // RUN) * P], U32, align_bytes=64)
+        x_scales = keep.tile([P, (HIDDEN // RUN) * P], U8, align_bytes=64)
+        latent_sums = latent_psum.tile([P, 4, P], F32)
+        latent_grouped = keep.tile([P, P, 4], BF16, align_bytes=64)
+        latent_codes = keep.tile([P, P], U32, align_bytes=64)
+        latent_scales = keep.tile([P, P], U8, align_bytes=64)
+        cos_table = keep.tile([P, KEY_HALF // 2], BF16)
+        sin_table = keep.tile([P, KEY_HALF // 2], BF16)
+
+        down_rows = Wkv_down.rearrange("(u p e) h -> u e p h", u=2, e=2)
+        key_rows = Wk_up.rearrange("(a c r j) l -> c r a j l", a=2, c=4, j=4)
+        value_rows = Wv_up.rearrange("(c a r j) l -> c r a j l", a=2, r=P, j=4)
+        stream = [("x", 0, i) for i in range(HIDDEN // CHUNK)]
+        stream += [("down", t, i) for t in range(4) for i in range(HIDDEN // CHUNK)]
+        for c in range(4):
+            stream += [("key", c, 0), ("value", 2 * c, 0), ("value", 2 * c + 1, 0)]
+        raw_tiles = {}
+        quantised = {}
+
+        def load(n):
+            kind, which, i = stream[n]
+            raw = raw_pool.tile([P, CHUNK], BF16, name="raw")
+            raw_tiles[n] = raw
+            columns = slice(i * CHUNK, (i + 1) * CHUNK)
+            if kind == "x":
+                for b in range(BATCH):
+                    nc.sync.dma_start(out=raw[b:P:BATCH, :], in_=hidden_states[b, :, columns])
+            elif kind == "down":
+                nc.sync.dma_start(out=raw[:], in_=down_rows[which // 2, which % 2][:, columns])
+            else:
+                rows = key_rows if kind == "key" else value_rows
+                nc.sync.dma_start(out=raw[:].rearrange("r (a j l) -> r a j l", a=2, j=4), in_=rows[which])
+
+        def transpose_and_quantise(raw, codes, scales, vector_helps):
+            words = raw[:].bitcast(F32)
+            for half in range(2):
+                grouped = grouped_pool.tile([P, CHUNK // 2], BF16, align_bytes=64, name="grouped")
+                grouped_words = grouped[:].bitcast(F32)
+                for bank in range(2):
+                    first = (2 * half + bank) * BANK_WORDS
+                    turned = turned_psum.tile([P, 4, P], F32, tag="turned")
+                    for q in range(4):
+                        nc.tensor.transpose(turned[:, q, :], words[:, first + q * P : first + (q + 1) * P], ident[:])
+                    side_by_side = grouped_words[:, bank * BANK_WORDS : (bank + 1) * BANK_WORDS].rearrange(
+                        "p (n r u) -> p n r u", n=2, u=2
+                    )
+                    planes = turned[:].rearrange("p (n u) r -> p n r u", u=2)
+                    if vector_helps and half == 1 and bank == 1:
+                        nc.vector.tensor_copy(out=side_by_side, in_=planes)
+                    else:
+                        nc.scalar.copy(out=side_by_side, in_=planes)
+                columns = slice(half * (CHUNK // 8), (half + 1) * (CHUNK // 8))
+                nc.vector.quantize_mx(out=codes[:, columns].bitcast(FP8X4), scales=scales[:, columns], in_=grouped[:])
+
+        def spread_bias(table_rows):
+            spread = turned_psum.tile([P, 4, P], F32, tag="turned")
+            for q, m in enumerate(table_rows):
+                nc.tensor.transpose(spread[:, q, :], bias_columns[:, m : m + 1].to_broadcast([P, P]), ident[:])
+            bias = bias_pool.tile([P, 4 * BIAS_ROW], BF16, name="bias")
+            nc.scalar.copy(out=bias[:].bitcast(F32), in_=spread[:].rearrange("p q w -> p (q w)"))
+            return bias
+
+        def prepare(n):
+            kind, which, i = stream[n]
+            raw = raw_tiles[n]
+            if kind == "x":
+                columns = slice(i * RUNS * P, (i + 1) * RUNS * P)
+                transpose_and_quantise(raw, x_codes[:, columns], x_scales[:, columns], True)
+                return
+            codes = code_pool.tile([P, RUNS * P], U32, align_bytes=64, name="codes")
+            scales = code_pool.tile([P, RUNS * P], U8, align_bytes=64, name="scales")
+            transpose_and_quantise(raw, codes[:], scales[:], kind == "down")
+            bias = None
+            if kind == "key":
+                low = key_bias_row + 2 * which
+                high = low + KEY_HALF // 2 // BIAS_ROW
+                bias = spread_bias([low, low + 1, high, high + 1])
+            elif kind == "value":
+                low = value_bias_row + 4 * which
+                bias = spread_bias([low, low + 1, low + 2, low + 3])
+            quantised[n] = (codes, scales, bias)
+
+        def multiply_down(t, i, codes, scales):
+            for n in range(RUNS):
+                g = i * RUNS + n
+                nc.tensor.matmul_mx(
+                    out=latent_sums[:, t, :],
+                    lhsT=codes[:, n * P : (n + 1) * P].bitcast(FP8X4),
+                    lhsT_scale=scales[:, n * P : (n + 1) * P],
+                    rhs=x_codes[:, g * P : (g + 1) * P].bitcast(FP8X4),
+                    rhs_scale=x_scales[:, g * P : (g + 1) * P],
+                    start=(g == 0),
+                    stop=(g == HIDDEN // RUN - 1),
+                )
+
+        def quantise_latent():
+            nc.vector.tensor_tensor(
+                out=latent_grouped[:],
+                in0=latent_sums[:].rearrange("p t k -> p k t"),
+                in1=latent_bias[:].unsqueeze(1).to_broadcast([P, P, 4]),
+                op=ADD,
+            )
+            nc.vector.quantize_mx(
+                out=latent_codes[:].bitcast(FP8X4),
+                scales=latent_scales[:],
+                in_=latent_grouped[:].rearrange("p k t -> p (k t)"),
+            )
+
+        def multiply_up(codes, scales, bias, result):
+            for a in range(2):
+                columns = slice(a * HEAD, (a + 1) * HEAD)
+                product = product_psum.tile([P, HEAD], F32, name="product")
+                nc.tensor.matmul_mx(
+                    out=product[:],
+                    lhsT=latent_codes[:].bitcast(FP8X4),
+                    lhsT_scale=latent_scales[:],
+                    rhs=codes[:, columns].bitcast(FP8X4),
+                    rhs_scale=scales[:, columns],
+                    start=True,
+                    stop=True,
+                )
+                nc.vector.tensor_tensor(
+                    out=result[:, a, :].rearrange("p (r j) -> p r j", j=4),
+                    in0=product[:].rearrange("p (j r) -> p r j", j=4),
+                    in1=bias[:, columns].rearrange("p (r j) -> p r j", j=4),
+                    op=ADD,
+                )
+
+        def multiply(n):
+            kind, which, i = stream[n]
+            if kind == "x":
+                return
+            codes, scales, bias = quantised[n]
+            if kind == "down":
+                multiply_down(which, i, codes, scales)
+                if which == 3 and i == HIDDEN // CHUNK - 1:
+                    quantise_latent()
+            elif kind == "key":
+                heads = key_pool.tile([P, 4, HEAD], F32, name="heads")
+                multiply_up(codes, scales, bias, heads[:, 0:2, :])
+                columns = slice(which * HEAD, (which + 1) * HEAD)
+                by_cos = key_pool.tile([P, 2, HEAD], F32, name="by_cos")
+                by_sin = key_pool.tile([P, 2, HEAD], F32, name="by_sin")
+                nc.vector.tensor_tensor(
+                    out=by_cos[:],
+                    in0=heads[:, 0:2, :],
+                    in1=cos_table[:, columns].unsqueeze(1).to_broadcast([P, 2, HEAD]),
+                    op=MULT,
+                )
+                nc.vector.tensor_tensor(
+                    out=by_sin[:],
+                    in0=heads[:, 0:2, :],
+                    in1=sin_table[:, columns].unsqueeze(1).to_broadcast([P, 2, HEAD]),
+                    op=MULT,
+                )
+                nc.vector.tensor_tensor(out=heads[:, 2, :], in0=by_cos[:, 0, :], in1=by_sin[:, 1, :], op=SUBTRACT)
+                nc.vector.tensor_tensor(out=heads[:, 3, :], in0=by_sin[:, 0, :], in1=by_cos[:, 1, :], op=ADD)
+                for b in range(BATCH):
+                    nc.sync.dma_start(
+                        out=out_0[b].rearrange("(q c) s d -> c s q d", q=4)[which], in_=heads[b:P:BATCH, :, :]
+                    )
+            else:
+                heads = value_pool.tile([P, 2, HEAD], F32, name="value_heads")
+                multiply_up(codes, scales, bias, heads[:])
+                for b in range(BATCH):
+                    nc.sync.dma_start(
+                        out=out_1[b, 2 * which : 2 * which + 2].rearrange("h s d -> s h d"),
+                        in_=heads[b:P:BATCH, :, :],
+                    )
+
+        for n in range(LOAD_AHEAD):
+            load(n)
+        for b in range(BATCH):
+            nc.sync.dma_start(out=cos_table[b:P:BATCH, :], in_=rope_cos)
+            nc.sync.dma_start(out=sin_table[b:P:BATCH, :], in_=rope_sin)
+        for n in range(len(stream) + LAG):
+            if n + LOAD_AHEAD < len(stream):
+                load(n + LOAD_AHEAD)
+            if n < len(stream):
+                prepare(n)
+            if n >= LAG:
+                multiply(n - LAG)

@@ -23,7 +23,7 @@ RUNS = CHUNK // RUN
 BANK_WORDS = 512
 BIAS_ROW = 256
 LOAD_AHEAD = 12
-LAG = 1
+LAG = 2
 
 FLOPS = 2 * BATCH * SEQ * (HIDDEN * LATENT + LATENT * (KEY_HALF + VALUE))
 
@@ -33,16 +33,17 @@ def tile_multiheadlatentattention_pb_k_kernel(
 ):
     nc = tc.nc
     with ExitStack() as ctx:
+        ctx.enter_context(tc.manual_schedule())
         keep = ctx.enter_context(tc.tile_pool(name="keep", bufs=1))
         raw_pool = ctx.enter_context(tc.tile_pool(name="raw", bufs=LOAD_AHEAD))
-        grouped_pool = ctx.enter_context(tc.tile_pool(name="grouped", bufs=4))
-        code_pool = ctx.enter_context(tc.tile_pool(name="codes", bufs=3))
-        bias_pool = ctx.enter_context(tc.tile_pool(name="bias", bufs=3))
+        grouped_pool = ctx.enter_context(tc.tile_pool(name="grouped", bufs=3))
+        code_pool = ctx.enter_context(tc.tile_pool(name="codes", bufs=LAG + 2))
+        bias_pool = ctx.enter_context(tc.tile_pool(name="bias", bufs=LAG + 2))
         key_pool = ctx.enter_context(tc.tile_pool(name="key", bufs=2))
         value_pool = ctx.enter_context(tc.tile_pool(name="value", bufs=3))
-        turned_psum = ctx.enter_context(tc.psum_pool(name="turned", bufs=4))
+        turned_psum = ctx.enter_context(tc.psum_pool(name="turned", bufs=5))
         latent_psum = ctx.enter_context(tc.psum_pool(name="latent", bufs=1))
-        product_psum = ctx.enter_context(tc.psum_pool(name="product", bufs=3))
+        product_psum = ctx.enter_context(tc.psum_pool(name="product", bufs=2))
 
         ident = keep.tile([P, P], F32)
         make_identity(nc, ident[:])
@@ -62,14 +63,16 @@ def tile_multiheadlatentattention_pb_k_kernel(
             out=bias_table[latent_bias_row : latent_bias_row + LATENT // BIAS_ROW, :],
             in_=bkv_down.rearrange("(m c) -> m c", c=BIAS_ROW),
         )
-        table_turned = turned_psum.tile([P, 4, P], F32, tag="turned")
-        nc.tensor.transpose(table_turned[:, 0, :], bias_table[:].bitcast(F32), ident[:])
         bias_columns = keep.tile([P, P], F32)
-        nc.vector.tensor_copy(out=bias_columns[:], in_=table_turned[:, 0, :])
         latent_bias = keep.tile([P, 4], F32)
-        nc.vector.tensor_copy(
-            out=latent_bias[:], in_=bias_columns[:, latent_bias_row : latent_bias_row + 2].bitcast(BF16)
-        )
+
+        def turn_bias_table():
+            table_turned = turned_psum.tile([P, 4, P], F32, tag="turned")
+            nc.tensor.transpose(table_turned[:, 0, :], bias_table[:].bitcast(F32), ident[:])
+            nc.vector.tensor_copy(out=bias_columns[:], in_=table_turned[:, 0, :])
+            nc.vector.tensor_copy(
+                out=latent_bias[:], in_=bias_columns[:, latent_bias_row : latent_bias_row + 2].bitcast(BF16)
+            )
 
         x_codes = keep.tile([P, (HIDDEN // RUN) * P], U32, align_bytes=64)
         x_scales = keep.tile([P, (HIDDEN // RUN) * P], U8, align_bytes=64)
@@ -85,6 +88,7 @@ def tile_multiheadlatentattention_pb_k_kernel(
         value_rows = Wv_up.rearrange("(c a r j) l -> c r a j l", a=2, r=P, j=4)
         stream = [("x", 0, i) for i in range(HIDDEN // CHUNK)]
         stream += [("down", t, i) for t in range(4) for i in range(HIDDEN // CHUNK)]
+        first_weight = HIDDEN // CHUNK
         for c in range(4):
             stream += [("key", c, 0), ("value", 2 * c, 0), ("value", 2 * c + 1, 0)]
         raw_tiles = {}
@@ -106,24 +110,31 @@ def tile_multiheadlatentattention_pb_k_kernel(
 
         def transpose_and_quantise(raw, codes, scales, vector_helps):
             words = raw[:].bitcast(F32)
+            banks = []
+            for bank in range(CHUNK // 2 // BANK_WORDS):
+                turned = turned_psum.tile([P, 4, P], F32, tag="turned")
+                for q in range(4):
+                    first = bank * BANK_WORDS + q * P
+                    nc.tensor.transpose(turned[:, q, :], words[:, first : first + P], ident[:])
+                banks.append(turned)
+            grouped = grouped_pool.tile([P, CHUNK], BF16, align_bytes=64, name="grouped")
+            grouped_words = grouped[:].bitcast(F32)
+            for bank, turned in enumerate(banks):
+                side_by_side = grouped_words[:, bank * BANK_WORDS : (bank + 1) * BANK_WORDS].rearrange(
+                    "p (n r u) -> p n r u", n=2, u=2
+                )
+                planes = turned[:].rearrange("p (n u) r -> p n r u", u=2)
+                if vector_helps and bank == 2:
+                    nc.vector.tensor_copy(out=side_by_side, in_=planes)
+                else:
+                    nc.scalar.copy(out=side_by_side, in_=planes)
             for half in range(2):
-                grouped = grouped_pool.tile([P, CHUNK // 2], BF16, align_bytes=64, name="grouped")
-                grouped_words = grouped[:].bitcast(F32)
-                for bank in range(2):
-                    first = (2 * half + bank) * BANK_WORDS
-                    turned = turned_psum.tile([P, 4, P], F32, tag="turned")
-                    for q in range(4):
-                        nc.tensor.transpose(turned[:, q, :], words[:, first + q * P : first + (q + 1) * P], ident[:])
-                    side_by_side = grouped_words[:, bank * BANK_WORDS : (bank + 1) * BANK_WORDS].rearrange(
-                        "p (n r u) -> p n r u", n=2, u=2
-                    )
-                    planes = turned[:].rearrange("p (n u) r -> p n r u", u=2)
-                    if vector_helps and half == 1 and bank == 1:
-                        nc.vector.tensor_copy(out=side_by_side, in_=planes)
-                    else:
-                        nc.scalar.copy(out=side_by_side, in_=planes)
                 columns = slice(half * (CHUNK // 8), (half + 1) * (CHUNK // 8))
-                nc.vector.quantize_mx(out=codes[:, columns].bitcast(FP8X4), scales=scales[:, columns], in_=grouped[:])
+                nc.vector.quantize_mx(
+                    out=codes[:, columns].bitcast(FP8X4),
+                    scales=scales[:, columns],
+                    in_=grouped[:, half * (CHUNK // 2) : (half + 1) * (CHUNK // 2)],
+                )
 
         def spread_bias(table_rows):
             spread = turned_psum.tile([P, 4, P], F32, tag="turned")
@@ -201,8 +212,6 @@ def tile_multiheadlatentattention_pb_k_kernel(
 
         def multiply(n):
             kind, which, i = stream[n]
-            if kind == "x":
-                return
             codes, scales, bias = quantised[n]
             if kind == "down":
                 multiply_down(which, i, codes, scales)
@@ -251,5 +260,7 @@ def tile_multiheadlatentattention_pb_k_kernel(
                 load(n + LOAD_AHEAD)
             if n < len(stream):
                 prepare(n)
-            if n >= LAG:
+            if n == first_weight:
+                turn_bias_table()
+            if n - LAG >= first_weight:
                 multiply(n - LAG)

@@ -23,7 +23,7 @@ RUNS = CHUNK // RUN
 BANK_WORDS = 512
 BIAS_ROW = 256
 LOAD_AHEAD = 12
-LAG = 2
+LAG = 1
 
 FLOPS = 2 * BATCH * SEQ * (HIDDEN * LATENT + LATENT * (KEY_HALF + VALUE))
 
@@ -42,8 +42,7 @@ def tile_multiheadlatentattention_pb_k_kernel(
         key_pool = ctx.enter_context(tc.tile_pool(name="key", bufs=2))
         value_pool = ctx.enter_context(tc.tile_pool(name="value", bufs=3))
         turned_psum = ctx.enter_context(tc.psum_pool(name="turned", bufs=5))
-        latent_psum = ctx.enter_context(tc.psum_pool(name="latent", bufs=1))
-        product_psum = ctx.enter_context(tc.psum_pool(name="product", bufs=2))
+        product_psum = ctx.enter_context(tc.psum_pool(name="product", bufs=3))
 
         ident = keep.tile([P, P], F32)
         make_identity(nc, ident[:])
@@ -76,7 +75,7 @@ def tile_multiheadlatentattention_pb_k_kernel(
 
         x_codes = keep.tile([P, (HIDDEN // RUN) * P], U32, align_bytes=64)
         x_scales = keep.tile([P, (HIDDEN // RUN) * P], U8, align_bytes=64)
-        latent_sums = latent_psum.tile([P, 4, P], F32)
+        latent_sums = product_psum.tile([P, 4, P], F32, tag="product")
         latent_grouped = keep.tile([P, P, 4], BF16, align_bytes=64)
         latent_codes = keep.tile([P, P], U32, align_bytes=64)
         latent_scales = keep.tile([P, P], U8, align_bytes=64)
@@ -193,7 +192,7 @@ def tile_multiheadlatentattention_pb_k_kernel(
         def multiply_up(codes, scales, bias, result):
             for a in range(2):
                 columns = slice(a * HEAD, (a + 1) * HEAD)
-                product = product_psum.tile([P, HEAD], F32, name="product")
+                product = product_psum.tile([P, HEAD], F32, tag="product")
                 nc.tensor.matmul_mx(
                     out=product[:],
                     lhsT=latent_codes[:].bitcast(FP8X4),

@@ -24,6 +24,9 @@ BANK_WORDS = 512
 BIAS_ROW = 256
 LOAD_AHEAD = 12
 LAG = 1
+WARM_UP = 5
+KEEP_X = 2
+KEEP = 1
 
 FLOPS = 2 * BATCH * SEQ * (HIDDEN * LATENT + LATENT * (KEY_HALF + VALUE))
 
@@ -39,10 +42,33 @@ def tile_multiheadlatentattention_pb_k_kernel(
         grouped_pool = ctx.enter_context(tc.tile_pool(name="grouped", bufs=3))
         code_pool = ctx.enter_context(tc.tile_pool(name="codes", bufs=LAG + 2))
         bias_pool = ctx.enter_context(tc.tile_pool(name="bias", bufs=LAG + 2))
-        key_pool = ctx.enter_context(tc.tile_pool(name="key", bufs=2))
-        value_pool = ctx.enter_context(tc.tile_pool(name="value", bufs=3))
-        turned_psum = ctx.enter_context(tc.psum_pool(name="turned", bufs=5))
+        key_pool = ctx.enter_context(tc.tile_pool(name="key", bufs=3))
+        value_pool = ctx.enter_context(tc.tile_pool(name="value", bufs=4))
+        rotate_pool = ctx.enter_context(tc.tile_pool(name="rotate", bufs=2))
+        turned_psum = ctx.enter_context(tc.psum_pool(name="turned", bufs=4))
         product_psum = ctx.enter_context(tc.psum_pool(name="product", bufs=3))
+        idle_psum = ctx.enter_context(tc.psum_pool(name="idle", bufs=1))
+
+        idle_codes = keep.tile([P, HEAD], U32, align_bytes=64)
+        idle_scales = keep.tile([P, HEAD], U8, align_bytes=64)
+        idle_sums = idle_psum.tile([P, HEAD], F32)
+        idle_values = keep.tile([P, 4 * HEAD], BF16, align_bytes=64)
+        nc.vector.memset(idle_values[:], 1.0)
+        nc.vector.quantize_mx(out=idle_codes[:].bitcast(FP8X4), scales=idle_scales[:], in_=idle_values[:])
+
+        def keep_clock(passes):
+            for extra in range(passes):
+                nc.tensor.matmul_mx(
+                    out=idle_sums[:],
+                    lhsT=idle_codes[:, 0:P].bitcast(FP8X4),
+                    lhsT_scale=idle_scales[:, 0:P],
+                    rhs=idle_codes[:].bitcast(FP8X4),
+                    rhs_scale=idle_scales[:],
+                    start=True,
+                    stop=True,
+                )
+
+        keep_clock(WARM_UP)
 
         ident = keep.tile([P, P], F32)
         make_identity(nc, ident[:])
@@ -149,6 +175,7 @@ def tile_multiheadlatentattention_pb_k_kernel(
             if kind == "x":
                 columns = slice(i * RUNS * P, (i + 1) * RUNS * P)
                 transpose_and_quantise(raw, x_codes[:, columns], x_scales[:, columns], True)
+                keep_clock(KEEP_X)
                 return
             codes = code_pool.tile([P, RUNS * P], U32, align_bytes=64, name="codes")
             scales = code_pool.tile([P, RUNS * P], U8, align_bytes=64, name="scales")
@@ -161,6 +188,7 @@ def tile_multiheadlatentattention_pb_k_kernel(
             elif kind == "value":
                 low = value_bias_row + 4 * which
                 bias = spread_bias([low, low + 1, low + 2, low + 3])
+            keep_clock(KEEP)
             quantised[n] = (codes, scales, bias)
 
         def multiply_down(t, i, codes, scales):
@@ -220,8 +248,8 @@ def tile_multiheadlatentattention_pb_k_kernel(
                 heads = key_pool.tile([P, 4, HEAD], F32, name="heads")
                 multiply_up(codes, scales, bias, heads[:, 0:2, :])
                 columns = slice(which * HEAD, (which + 1) * HEAD)
-                by_cos = key_pool.tile([P, 2, HEAD], F32, name="by_cos")
-                by_sin = key_pool.tile([P, 2, HEAD], F32, name="by_sin")
+                by_cos = rotate_pool.tile([P, 2, HEAD], F32, name="by_cos")
+                by_sin = rotate_pool.tile([P, 2, HEAD], F32, name="by_sin")
                 nc.vector.tensor_tensor(
                     out=by_cos[:],
                     in0=heads[:, 0:2, :],

@@ -7,6 +7,7 @@ F32 = mybir.dt.float32
 BF16 = mybir.dt.bfloat16
 U32 = mybir.dt.uint32
 U8 = mybir.dt.uint8
+I32 = mybir.dt.int32
 FP8X4 = mybir.dt.float8_e4m3fn_x4
 ADD = mybir.AluOpType.add
 SUBTRACT = mybir.AluOpType.subtract
@@ -53,7 +54,7 @@ def tile_multiheadlatentattention_pb_k_kernel(
         idle_scales = keep.tile([P, HEAD], U8, align_bytes=64)
         idle_sums = idle_psum.tile([P, HEAD], F32)
         idle_values = keep.tile([P, 4 * HEAD], BF16, align_bytes=64)
-        nc.vector.memset(idle_values[:], 1.0)
+        nc.vector.memset(idle_values[:].bitcast(I32), 0)
         nc.vector.quantize_mx(out=idle_codes[:].bitcast(FP8X4), scales=idle_scales[:], in_=idle_values[:])
 
         def keep_clock(passes):
@@ -114,8 +115,10 @@ def tile_multiheadlatentattention_pb_k_kernel(
         stream = [("x", 0, i) for i in range(HIDDEN // CHUNK)]
         stream += [("down", t, i) for t in range(4) for i in range(HIDDEN // CHUNK)]
         first_weight = HIDDEN // CHUNK
-        for c in range(4):
-            stream += [("key", c, 0), ("value", 2 * c, 0), ("value", 2 * c + 1, 0)]
+        stream += [("key", 0, 0)]
+        for c in range(1, 4):
+            stream += [("value", 2 * c - 2, 0), ("key", c, 0), ("value", 2 * c - 1, 0)]
+        stream += [("value", 6, 0), ("value", 7, 0)]
         raw_tiles = {}
         quantised = {}
 
@@ -237,6 +240,9 @@ def tile_multiheadlatentattention_pb_k_kernel(
                     op=ADD,
                 )
 
+        def key_heads(b, c):
+            return out_0[b].rearrange("(q c) s d -> c s q d", q=4)[c]
+
         def multiply(n):
             kind, which, i = stream[n]
             codes, scales, bias = quantised[n]
@@ -247,6 +253,8 @@ def tile_multiheadlatentattention_pb_k_kernel(
             elif kind == "key":
                 heads = key_pool.tile([P, 4, HEAD], F32, name="heads")
                 multiply_up(codes, scales, bias, heads[:, 0:2, :])
+                for b in range(BATCH):
+                    nc.sync.dma_start(out=key_heads(b, which)[:, 0:2, :], in_=heads[b:P:BATCH, 0:2, :])
                 columns = slice(which * HEAD, (which + 1) * HEAD)
                 by_cos = rotate_pool.tile([P, 2, HEAD], F32, name="by_cos")
                 by_sin = rotate_pool.tile([P, 2, HEAD], F32, name="by_sin")
@@ -262,12 +270,10 @@ def tile_multiheadlatentattention_pb_k_kernel(
                     in1=sin_table[:, columns].unsqueeze(1).to_broadcast([P, 2, HEAD]),
                     op=MULT,
                 )
-                nc.vector.tensor_tensor(out=heads[:, 2, :], in0=by_cos[:, 0, :], in1=by_sin[:, 1, :], op=SUBTRACT)
-                nc.vector.tensor_tensor(out=heads[:, 3, :], in0=by_sin[:, 0, :], in1=by_cos[:, 1, :], op=ADD)
+                nc.gpsimd.tensor_tensor(out=heads[:, 2, :], in0=by_cos[:, 0, :], in1=by_sin[:, 1, :], op=SUBTRACT)
+                nc.gpsimd.tensor_tensor(out=heads[:, 3, :], in0=by_sin[:, 0, :], in1=by_cos[:, 1, :], op=ADD)
                 for b in range(BATCH):
-                    nc.sync.dma_start(
-                        out=out_0[b].rearrange("(q c) s d -> c s q d", q=4)[which], in_=heads[b:P:BATCH, :, :]
-                    )
+                    nc.gpsimd.dma_start(out=key_heads(b, which)[:, 2:4, :], in_=heads[b:P:BATCH, 2:4, :])
             else:
                 heads = value_pool.tile([P, 2, HEAD], F32, name="value_heads")
                 multiply_up(codes, scales, bias, heads[:])

@@ -128,8 +128,7 @@ def tile_multiheadlatentattention_pb_k_kernel(
             raw_tiles[n] = raw
             columns = slice(i * CHUNK, (i + 1) * CHUNK)
             if kind == "x":
-                for b in range(BATCH):
-                    nc.sync.dma_start(out=raw[b:P:BATCH, :], in_=hidden_states[b, :, columns])
+                nc.sync.dma_start(out=raw[:], in_=hidden_states[:, :, columns].rearrange("b s h -> s b h"))
             elif kind == "down":
                 nc.sync.dma_start(out=raw[:], in_=down_rows[which // 2, which % 2][:, columns])
             else:
@@ -240,8 +239,8 @@ def tile_multiheadlatentattention_pb_k_kernel(
                     op=ADD,
                 )
 
-        def key_heads(b, c):
-            return out_0[b].rearrange("(q c) s d -> c s q d", q=4)[c]
+        def head_rows(out, h):
+            return out[:, h].rearrange("b s d -> s b d")
 
         def multiply(n):
             kind, which, i = stream[n]
@@ -253,8 +252,8 @@ def tile_multiheadlatentattention_pb_k_kernel(
             elif kind == "key":
                 heads = key_pool.tile([P, 4, HEAD], F32, name="heads")
                 multiply_up(codes, scales, bias, heads[:, 0:2, :])
-                for b in range(BATCH):
-                    nc.sync.dma_start(out=key_heads(b, which)[:, 0:2, :], in_=heads[b:P:BATCH, 0:2, :])
+                for q in range(2):
+                    nc.sync.dma_start(out=head_rows(out_0, 4 * q + which), in_=heads[:, q, :])
                 columns = slice(which * HEAD, (which + 1) * HEAD)
                 by_cos = rotate_pool.tile([P, 2, HEAD], F32, name="by_cos")
                 by_sin = rotate_pool.tile([P, 2, HEAD], F32, name="by_sin")
@@ -272,16 +271,13 @@ def tile_multiheadlatentattention_pb_k_kernel(
                 )
                 nc.gpsimd.tensor_tensor(out=heads[:, 2, :], in0=by_cos[:, 0, :], in1=by_sin[:, 1, :], op=SUBTRACT)
                 nc.gpsimd.tensor_tensor(out=heads[:, 3, :], in0=by_sin[:, 0, :], in1=by_cos[:, 1, :], op=ADD)
-                for b in range(BATCH):
-                    nc.gpsimd.dma_start(out=key_heads(b, which)[:, 2:4, :], in_=heads[b:P:BATCH, 2:4, :])
+                for q in range(2, 4):
+                    nc.gpsimd.dma_start(out=head_rows(out_0, 4 * q + which), in_=heads[:, q, :])
             else:
                 heads = value_pool.tile([P, 2, HEAD], F32, name="value_heads")
                 multiply_up(codes, scales, bias, heads[:])
-                for b in range(BATCH):
-                    nc.sync.dma_start(
-                        out=out_1[b, 2 * which : 2 * which + 2].rearrange("h s d -> s h d"),
-                        in_=heads[b:P:BATCH, :, :],
-                    )
+                for q in range(2):
+                    nc.sync.dma_start(out=head_rows(out_1, 2 * which + q), in_=heads[:, q, :])
 
         for n in range(LOAD_AHEAD):
             load(n)

@@ -78,17 +78,20 @@ def tile_multiheadlatentattention_pb_k_kernel(
         value_bias_row = KEY_HALF // BIAS_ROW
         latent_bias_row = value_bias_row + VALUE // BIAS_ROW
         bias_table = keep.tile([P, BIAS_ROW], BF16)
-        nc.vector.memset(bias_table[:], 0.0)
-        nc.scalar.dma_start(
-            out=bias_table[key_bias_row:value_bias_row, :], in_=bk_up.rearrange("(m c) -> m c", c=BIAS_ROW)
-        )
-        nc.scalar.dma_start(
-            out=bias_table[value_bias_row:latent_bias_row, :], in_=bv_up.rearrange("(m c) -> m c", c=BIAS_ROW)
-        )
-        nc.scalar.dma_start(
-            out=bias_table[latent_bias_row : latent_bias_row + LATENT // BIAS_ROW, :],
-            in_=bkv_down.rearrange("(m c) -> m c", c=BIAS_ROW),
-        )
+        nc.gpsimd.memset(bias_table[:], 0.0)
+
+        def load_biases():
+            nc.sync.dma_start(
+                out=bias_table[key_bias_row:value_bias_row, :], in_=bk_up.rearrange("(m c) -> m c", c=BIAS_ROW)
+            )
+            nc.sync.dma_start(
+                out=bias_table[value_bias_row:latent_bias_row, :], in_=bv_up.rearrange("(m c) -> m c", c=BIAS_ROW)
+            )
+            nc.sync.dma_start(
+                out=bias_table[latent_bias_row : latent_bias_row + LATENT // BIAS_ROW, :],
+                in_=bkv_down.rearrange("(m c) -> m c", c=BIAS_ROW),
+            )
+
         bias_columns = keep.tile([P, P], F32)
         latent_bias = keep.tile([P, 4], F32)
 
@@ -190,7 +193,8 @@ def tile_multiheadlatentattention_pb_k_kernel(
             elif kind == "value":
                 low = value_bias_row + 4 * which
                 bias = spread_bias([low, low + 1, low + 2, low + 3])
-            keep_clock(KEEP)
+            if kind != "down":
+                keep_clock(KEEP)
             quantised[n] = (codes, scales, bias)
 
         def multiply_down(t, i, codes, scales):
@@ -281,6 +285,8 @@ def tile_multiheadlatentattention_pb_k_kernel(
 
         for n in range(LOAD_AHEAD):
             load(n)
+            if n == first_weight - 1:
+                load_biases()
         for b in range(BATCH):
             nc.sync.dma_start(out=cos_table[b:P:BATCH, :], in_=rope_cos)
             nc.sync.dma_start(out=sin_table[b:P:BATCH, :], in_=rope_sin)

from contextlib import ExitStack

import concourse.mybir as mybir
from concourse.masks import make_identity

F32 = mybir.dt.float32
BF16 = mybir.dt.bfloat16
U32 = mybir.dt.uint32
U8 = mybir.dt.uint8
I32 = mybir.dt.int32
FP8X4 = mybir.dt.float8_e4m3fn_x4
ADD = mybir.AluOpType.add
SUBTRACT = mybir.AluOpType.subtract
MULT = mybir.AluOpType.mult

P = 128
BATCH, SEQ, HIDDEN, LATENT = 2, 64, 8192, 512
HEAD = 512
KEY_HALF = 4096
VALUE = 8192
CHUNK = 4096
RUN = 512
RUNS = CHUNK // RUN
BANK_WORDS = 512
BIAS_ROW = 256
LOAD_AHEAD = 12
LAG = 1
WARM_UP = 5
KEEP_X = 2
KEEP = 1

FLOPS = 2 * BATCH * SEQ * (HIDDEN * LATENT + LATENT * (KEY_HALF + VALUE))


def tile_multiheadlatentattention_pb_k_kernel(
    tc, hidden_states, Wkv_down, bkv_down, Wk_up, bk_up, Wv_up, bv_up, rope_cos, rope_sin, out_0, out_1
):
    nc = tc.nc
    with ExitStack() as ctx:
        ctx.enter_context(tc.manual_schedule())
        keep = ctx.enter_context(tc.tile_pool(name="keep", bufs=1))
        raw_pool = ctx.enter_context(tc.tile_pool(name="raw", bufs=LOAD_AHEAD))
        grouped_pool = ctx.enter_context(tc.tile_pool(name="grouped", bufs=3))
        code_pool = ctx.enter_context(tc.tile_pool(name="codes", bufs=LAG + 2))
        bias_pool = ctx.enter_context(tc.tile_pool(name="bias", bufs=LAG + 2))
        key_pool = ctx.enter_context(tc.tile_pool(name="key", bufs=3))
        value_pool = ctx.enter_context(tc.tile_pool(name="value", bufs=4))
        rotate_pool = ctx.enter_context(tc.tile_pool(name="rotate", bufs=2))
        turned_psum = ctx.enter_context(tc.psum_pool(name="turned", bufs=4))
        product_psum = ctx.enter_context(tc.psum_pool(name="product", bufs=3))
        idle_psum = ctx.enter_context(tc.psum_pool(name="idle", bufs=1))

        idle_codes = keep.tile([P, HEAD], U32, align_bytes=64)
        idle_scales = keep.tile([P, HEAD], U8, align_bytes=64)
        idle_sums = idle_psum.tile([P, HEAD], F32)
        idle_values = keep.tile([P, 4 * HEAD], BF16, align_bytes=64)
        nc.vector.memset(idle_values[:].bitcast(I32), 0)
        nc.vector.quantize_mx(out=idle_codes[:].bitcast(FP8X4), scales=idle_scales[:], in_=idle_values[:])

        def keep_clock(passes):
            for extra in range(passes):
                nc.tensor.matmul_mx(
                    out=idle_sums[:],
                    lhsT=idle_codes[:, 0:P].bitcast(FP8X4),
                    lhsT_scale=idle_scales[:, 0:P],
                    rhs=idle_codes[:].bitcast(FP8X4),
                    rhs_scale=idle_scales[:],
                    start=True,
                    stop=True,
                )

        keep_clock(WARM_UP)

        ident = keep.tile([P, P], F32)
        make_identity(nc, ident[:])

        key_bias_row = 0
        value_bias_row = KEY_HALF // BIAS_ROW
        latent_bias_row = value_bias_row + VALUE // BIAS_ROW
        bias_table = keep.tile([P, BIAS_ROW], BF16)
        nc.gpsimd.memset(bias_table[:], 0.0)

        def load_biases():
            nc.sync.dma_start(
                out=bias_table[key_bias_row:value_bias_row, :], in_=bk_up.rearrange("(m c) -> m c", c=BIAS_ROW)
            )
            nc.sync.dma_start(
                out=bias_table[value_bias_row:latent_bias_row, :], in_=bv_up.rearrange("(m c) -> m c", c=BIAS_ROW)
            )
            nc.sync.dma_start(
                out=bias_table[latent_bias_row : latent_bias_row + LATENT // BIAS_ROW, :],
                in_=bkv_down.rearrange("(m c) -> m c", c=BIAS_ROW),
            )

        bias_columns = keep.tile([P, P], F32)
        latent_bias = keep.tile([P, 4], F32)

        def turn_bias_table():
            table_turned = turned_psum.tile([P, 4, P], F32, tag="turned")
            nc.tensor.transpose(table_turned[:, 0, :], bias_table[:].bitcast(F32), ident[:])
            nc.vector.tensor_copy(out=bias_columns[:], in_=table_turned[:, 0, :])
            nc.vector.tensor_copy(
                out=latent_bias[:], in_=bias_columns[:, latent_bias_row : latent_bias_row + 2].bitcast(BF16)
            )

        x_codes = keep.tile([P, (HIDDEN // RUN) * P], U32, align_bytes=64)
        x_scales = keep.tile([P, (HIDDEN // RUN) * P], U8, align_bytes=64)
        latent_sums = product_psum.tile([P, 4, P], F32, tag="product")
        latent_grouped = keep.tile([P, P, 4], BF16, align_bytes=64)
        latent_codes = keep.tile([P, P], U32, align_bytes=64)
        latent_scales = keep.tile([P, P], U8, align_bytes=64)
        cos_table = keep.tile([P, KEY_HALF // 2], BF16)
        sin_table = keep.tile([P, KEY_HALF // 2], BF16)

        down_rows = Wkv_down.rearrange("(u p e) h -> u e p h", u=2, e=2)
        key_rows = Wk_up.rearrange("(a c r j) l -> c r a j l", a=2, c=4, j=4)
        value_rows = Wv_up.rearrange("(c a r j) l -> c r a j l", a=2, r=P, j=4)
        stream = [("x", 0, i) for i in range(HIDDEN // CHUNK)]
        stream += [("down", t, i) for t in range(4) for i in range(HIDDEN // CHUNK)]
        first_weight = HIDDEN // CHUNK
        stream += [("key", 0, 0)]
        for c in range(1, 4):
            stream += [("value", 2 * c - 2, 0), ("key", c, 0), ("value", 2 * c - 1, 0)]
        stream += [("value", 6, 0), ("value", 7, 0)]
        raw_tiles = {}
        quantised = {}

        def load(n):
            kind, which, i = stream[n]
            raw = raw_pool.tile([P, CHUNK], BF16, name="raw")
            raw_tiles[n] = raw
            columns = slice(i * CHUNK, (i + 1) * CHUNK)
            if kind == "x":
                nc.sync.dma_start(out=raw[:], in_=hidden_states[:, :, columns].rearrange("b s h -> s b h"))
            elif kind == "down":
                nc.sync.dma_start(out=raw[:], in_=down_rows[which // 2, which % 2][:, columns])
            else:
                rows = key_rows if kind == "key" else value_rows
                nc.sync.dma_start(out=raw[:].rearrange("r (a j l) -> r a j l", a=2, j=4), in_=rows[which])

        def transpose_and_quantise(raw, codes, scales, vector_helps):
            words = raw[:].bitcast(F32)
            banks = []
            for bank in range(CHUNK // 2 // BANK_WORDS):
                turned = turned_psum.tile([P, 4, P], F32, tag="turned")
                for q in range(4):
                    first = bank * BANK_WORDS + q * P
                    nc.tensor.transpose(turned[:, q, :], words[:, first : first + P], ident[:])
                banks.append(turned)
            grouped = grouped_pool.tile([P, CHUNK], BF16, align_bytes=64, name="grouped")
            grouped_words = grouped[:].bitcast(F32)
            for bank, turned in enumerate(banks):
                side_by_side = grouped_words[:, bank * BANK_WORDS : (bank + 1) * BANK_WORDS].rearrange(
                    "p (n r u) -> p n r u", n=2, u=2
                )
                planes = turned[:].rearrange("p (n u) r -> p n r u", u=2)
                if vector_helps and bank == 2:
                    nc.vector.tensor_copy(out=side_by_side, in_=planes)
                else:
                    nc.scalar.copy(out=side_by_side, in_=planes)
            for half in range(2):
                columns = slice(half * (CHUNK // 8), (half + 1) * (CHUNK // 8))
                nc.vector.quantize_mx(
                    out=codes[:, columns].bitcast(FP8X4),
                    scales=scales[:, columns],
                    in_=grouped[:, half * (CHUNK // 2) : (half + 1) * (CHUNK // 2)],
                )

        def spread_bias(table_rows):
            spread = turned_psum.tile([P, 4, P], F32, tag="turned")
            for q, m in enumerate(table_rows):
                nc.tensor.transpose(spread[:, q, :], bias_columns[:, m : m + 1].to_broadcast([P, P]), ident[:])
            bias = bias_pool.tile([P, 4 * BIAS_ROW], BF16, name="bias")
            nc.scalar.copy(out=bias[:].bitcast(F32), in_=spread[:].rearrange("p q w -> p (q w)"))
            return bias

        def prepare(n):
            kind, which, i = stream[n]
            raw = raw_tiles[n]
            if kind == "x":
                columns = slice(i * RUNS * P, (i + 1) * RUNS * P)
                transpose_and_quantise(raw, x_codes[:, columns], x_scales[:, columns], True)
                keep_clock(KEEP_X)
                return
            codes = code_pool.tile([P, RUNS * P], U32, align_bytes=64, name="codes")
            scales = code_pool.tile([P, RUNS * P], U8, align_bytes=64, name="scales")
            transpose_and_quantise(raw, codes[:], scales[:], kind == "down")
            bias = None
            if kind == "key":
                low = key_bias_row + 2 * which
                high = low + KEY_HALF // 2 // BIAS_ROW
                bias = spread_bias([low, low + 1, high, high + 1])
            elif kind == "value":
                low = value_bias_row + 4 * which
                bias = spread_bias([low, low + 1, low + 2, low + 3])
            if kind != "down":
                keep_clock(KEEP)
            quantised[n] = (codes, scales, bias)

        def multiply_down(t, i, codes, scales):
            for n in range(RUNS):
                g = i * RUNS + n
                nc.tensor.matmul_mx(
                    out=latent_sums[:, t, :],
                    lhsT=codes[:, n * P : (n + 1) * P].bitcast(FP8X4),
                    lhsT_scale=scales[:, n * P : (n + 1) * P],
                    rhs=x_codes[:, g * P : (g + 1) * P].bitcast(FP8X4),
                    rhs_scale=x_scales[:, g * P : (g + 1) * P],
                    start=(g == 0),
                    stop=(g == HIDDEN // RUN - 1),
                )

        def quantise_latent():
            nc.vector.tensor_tensor(
                out=latent_grouped[:],
                in0=latent_sums[:].rearrange("p t k -> p k t"),
                in1=latent_bias[:].unsqueeze(1).to_broadcast([P, P, 4]),
                op=ADD,
            )
            nc.vector.quantize_mx(
                out=latent_codes[:].bitcast(FP8X4),
                scales=latent_scales[:],
                in_=latent_grouped[:].rearrange("p k t -> p (k t)"),
            )

        def multiply_up(codes, scales, bias, result):
            for a in range(2):
                columns = slice(a * HEAD, (a + 1) * HEAD)
                product = product_psum.tile([P, HEAD], F32, tag="product")
                nc.tensor.matmul_mx(
                    out=product[:],
                    lhsT=latent_codes[:].bitcast(FP8X4),
                    lhsT_scale=latent_scales[:],
                    rhs=codes[:, columns].bitcast(FP8X4),
                    rhs_scale=scales[:, columns],
                    start=True,
                    stop=True,
                )
                nc.vector.tensor_tensor(
                    out=result[:, a, :].rearrange("p (r j) -> p r j", j=4),
                    in0=product[:].rearrange("p (j r) -> p r j", j=4),
                    in1=bias[:, columns].rearrange("p (r j) -> p r j", j=4),
                    op=ADD,
                )

        def head_rows(out, h):
            return out[:, h].rearrange("b s d -> s b d")

        def multiply(n):
            kind, which, i = stream[n]
            codes, scales, bias = quantised[n]
            if kind == "down":
                multiply_down(which, i, codes, scales)
                if which == 3 and i == HIDDEN // CHUNK - 1:
                    quantise_latent()
            elif kind == "key":
                heads = key_pool.tile([P, 4, HEAD], F32, name="heads")
                multiply_up(codes, scales, bias, heads[:, 0:2, :])
                for q in range(2):
                    nc.sync.dma_start(out=head_rows(out_0, 4 * q + which), in_=heads[:, q, :])
                columns = slice(which * HEAD, (which + 1) * HEAD)
                by_cos = rotate_pool.tile([P, 2, HEAD], F32, name="by_cos")
                by_sin = rotate_pool.tile([P, 2, HEAD], F32, name="by_sin")
                nc.vector.tensor_tensor(
                    out=by_cos[:],
                    in0=heads[:, 0:2, :],
                    in1=cos_table[:, columns].unsqueeze(1).to_broadcast([P, 2, HEAD]),
                    op=MULT,
                )
                nc.vector.tensor_tensor(
                    out=by_sin[:],
                    in0=heads[:, 0:2, :],
                    in1=sin_table[:, columns].unsqueeze(1).to_broadcast([P, 2, HEAD]),
                    op=MULT,
                )
                nc.gpsimd.tensor_tensor(out=heads[:, 2, :], in0=by_cos[:, 0, :], in1=by_sin[:, 1, :], op=SUBTRACT)
                nc.gpsimd.tensor_tensor(out=heads[:, 3, :], in0=by_sin[:, 0, :], in1=by_cos[:, 1, :], op=ADD)
                for q in range(2, 4):
                    nc.gpsimd.dma_start(out=head_rows(out_0, 4 * q + which), in_=heads[:, q, :])
            else:
                heads = value_pool.tile([P, 2, HEAD], F32, name="value_heads")
                multiply_up(codes, scales, bias, heads[:])
                for q in range(2):
                    nc.sync.dma_start(out=head_rows(out_1, 2 * which + q), in_=heads[:, q, :])

        for n in range(LOAD_AHEAD):
            load(n)
            if n == first_weight - 1:
                load_biases()
        for b in range(BATCH):
            nc.sync.dma_start(out=cos_table[b:P:BATCH, :], in_=rope_cos)
            nc.sync.dma_start(out=sin_table[b:P:BATCH, :], in_=rope_sin)
        for n in range(len(stream) + LAG):
            if n + LOAD_AHEAD < len(stream):
                load(n + LOAD_AHEAD)
            if n < len(stream):
                prepare(n)
            if n == first_weight:
                turn_bias_table()
            if n - LAG >= first_weight:
                multiply(n - LAG)
